import numpy as np
import ml_dtypes


def mxq(x, axis, fmt="e4m3"):
    dtype, down = {"e4m3": (ml_dtypes.float8_e4m3fn, 7), "e5m2": (ml_dtypes.float8_e5m2, 14)}[fmt]
    v = np.moveaxis(np.asarray(x, np.float32).astype(ml_dtypes.bfloat16).astype(np.float64), axis, -1)
    blocks = v.reshape(v.shape[:-1] + (-1, 32))
    amax = np.abs(blocks).max(-1, keepdims=True)
    byte = np.maximum(np.where(amax > 0, np.frexp(amax)[1] - 1 + 127, 0) - down, 1)
    scale = np.exp2(byte - 127.0)
    codes = (blocks / scale).astype(np.float32).astype(dtype).astype(np.float64)
    return np.moveaxis((codes * scale).reshape(v.shape), -1, axis)


WIDE = False


def mx_kscale(k):
    if not WIDE:
        return np.ones(k)
    levels = np.array([10, -10, 5, -5, 0])
    a = np.random.permutation(np.resize(levels, k // 512 * 4)).reshape(k // 512, 4)
    idx = np.arange(k)
    return np.exp2(a[idx // 512, idx % 128 // 32])


BF16 = ml_dtypes.bfloat16


def bf(x):
    return np.asarray(x, np.float32).astype(BF16)


def f64(x):
    return np.asarray(x).astype(np.float64)


Nc, Ns, Nt, d_h, BS = 64, 64, 16, 128, 1
I, J = Ns * Nt, Nc * Nt


def setup_inputs():
    s = mx_kscale(J)
    Ac = (np.random.random((Ns, Nc)) < 3.2 / Ns).astype(np.float64)
    Ac[np.random.randint(0, Ns, Nc), np.arange(Nc)] = 1.0
    Ac[np.arange(Ns), np.random.randint(0, Nc, Ns)] = 1.0
    As = (np.random.random((Ns, Ns)) < 0.05).astype(np.float64)
    AA = np.dot(np.dot(As, As), Ac) + np.dot(As, Ac) + Ac
    AA = (AA != 0).astype(np.float64)
    AA_mask = np.tile(AA, (Nt, Nt))
    g = 1.0 / np.sqrt(0.5 * J * AA.mean())
    GCW = np.random.standard_normal((I, J)) * g * s[None, :]
    GCB = np.random.standard_normal((I, d_h)) * 0.5
    h = np.random.standard_normal((BS, Nc, Nt, d_h)) / s.reshape(Nt, Nc).T[None, :, :, None]
    e = np.random.standard_normal(1) * 0.1
    return {"h": bf(h), "e": bf(e), "AA_mask": bf(AA_mask), "GCW": bf(GCW), "GCB": bf(GCB)}


def reference(h, e, AA_mask, GCW, GCB):
    bs = h.shape[0]
    A = np.maximum(f64(AA_mask) * f64(GCW), 0.0)
    x = np.transpose(f64(h), (0, 2, 1, 3)).reshape(bs, Nt * Nc, d_h)
    x = np.maximum((mxq(A, 1, "e4m3") @ mxq(x, 1, "e4m3")) + f64(GCB), 0.0)
    x = x.reshape(bs, Nt, Ns, d_h)
    x = np.transpose(x, (0, 2, 1, 3))
    return x

@@ -1,0 +1,123 @@
+from contextlib import ExitStack
+
+import concourse.mybir as mybir
+from concourse.masks import make_identity
+
+F32 = mybir.dt.float32
+BF16 = mybir.dt.bfloat16
+U32 = mybir.dt.uint32
+U8 = mybir.dt.uint8
+FP8X4 = mybir.dt.float8_e4m3fn_x4
+RELU = mybir.ActivationFunctionType.Relu
+MULT = mybir.AluOpType.mult
+ADD = mybir.AluOpType.add
+
+P = 128
+NODES = 64
+STEPS = 16
+FEATURES = 128
+K = NODES * STEPS
+ROWS = NODES * STEPS
+BLOCKS = ROWS // P
+PASSES = 2
+PLANES = 2
+
+FLOPS = 2 * ROWS * K * FEATURES
+
+
+def tile_gcnfast_s_kernel(tc, h, e, AA_mask, GCW, GCB, out):
+    nc = tc.nc
+    weight_rows = GCW.rearrange("(p j) k -> p j k", j=BLOCKS)
+    mask_rows = AA_mask.rearrange("(p j) k -> p j k", j=BLOCKS)
+    bias_rows = GCB.rearrange("(p j) d -> p j d", j=BLOCKS)
+    out_blocks = out[0].rearrange("(pl j) t d -> j t pl d", j=BLOCKS)
+
+    with ExitStack() as ctx:
+        keep = ctx.enter_context(tc.tile_pool(name="keep", bufs=1))
+        loads = ctx.enter_context(tc.tile_pool(name="loads", bufs=BLOCKS))
+        work = ctx.enter_context(tc.tile_pool(name="work", bufs=3))
+        flipped = ctx.enter_context(tc.psum_pool(name="flipped", bufs=6))
+        sums = ctx.enter_context(tc.psum_pool(name="sums", bufs=2))
+
+        x_raw = keep.tile([P, 2, 4 * FEATURES], BF16)
+        for tx in range(4):
+            nc.scalar.dma_start(
+                out=x_raw[32 * tx : 32 * tx + 32, :, :],
+                in_=h[0, :, 4 * tx : 4 * tx + 4, :].rearrange("(cp ce) tl d -> cp ce (tl d)", ce=2),
+            )
+        bias = keep.tile([P, BLOCKS, FEATURES], BF16)
+        nc.scalar.dma_start(out=bias[:], in_=bias_rows)
+        weight_tiles = []
+        mask_tiles = []
+        for j in range(BLOCKS):
+            weight = loads.tile([P, K], BF16)
+            nc.sync.dma_start(out=weight[:], in_=weight_rows[:, j, :])
+            mask = loads.tile([P, K], BF16)
+            nc.sync.dma_start(out=mask[:], in_=mask_rows[:, j, :])
+            weight_tiles.append(weight)
+            mask_tiles.append(mask)
+
+        identity = keep.tile([P, P], F32)
+        make_identity(nc, identity[:])
+
+        x_grouped = keep.tile([P, PASSES, FEATURES, 4], BF16, align_bytes=64)
+        x_steps = x_raw[:].rearrange("p ce (u q d) -> p q d u ce", u=PLANES, q=PASSES)
+        for q in range(PASSES):
+            nc.vector.tensor_copy(
+                out=x_grouped[:, q, :, :].rearrange("p d (u ce) -> p d u ce", ce=2),
+                in_=x_steps[:, q, :, :, :],
+            )
+        x_codes = keep.tile([P, PASSES, FEATURES], U32, align_bytes=64)
+        x_scales = keep.tile([P, PASSES, FEATURES], U8, align_bytes=64)
+        nc.vector.quantize_mx(
+            out=x_codes[:].rearrange("p q d -> p (q d)").bitcast(FP8X4),
+            scales=x_scales[:].rearrange("p q d -> p (q d)"),
+            in_=x_grouped[:].rearrange("p q d v -> p (q d v)"),
+        )
+
+        for j in range(BLOCKS):
+            product = work.tile([P, K], BF16)
+            nc.vector.tensor_tensor(
+                out=product[:].rearrange("p (tl tx c) -> p tx tl c", tl=4, tx=4),
+                in0=weight_tiles[j][:].rearrange("p (tx tl c) -> p tx tl c", tx=4, tl=4),
+                in1=mask_tiles[j][:].rearrange("p (tx tl c) -> p tx tl c", tx=4, tl=4),
+                op=MULT,
+            )
+            product_words = product[:].bitcast(F32)
+
+            a_grouped = work.tile([P, PASSES, P, 4], BF16, align_bytes=64)
+            for q in range(PASSES):
+                turned = flipped.tile([P, PLANES, P], F32)
+                for u in range(PLANES):
+                    tl = PASSES * u + q
+                    nc.tensor.transpose(
+                        turned[:, u, :], product_words[:, P * tl : P * tl + P], identity[:]
+                    )
+                nc.scalar.activation(
+                    out=a_grouped[:, q, :, :].rearrange("p r (u ce) -> p r u ce", ce=2),
+                    in_=turned[:].bitcast(BF16).rearrange("p u (r ce) -> p r u ce", ce=2),
+                    func=RELU,
+                )
+            a_codes = work.tile([P, PASSES, P], U32, align_bytes=64)
+            a_scales = work.tile([P, PASSES, P], U8, align_bytes=64)
+            nc.vector.quantize_mx(
+                out=a_codes[:].rearrange("p q r -> p (q r)").bitcast(FP8X4),
+                scales=a_scales[:].rearrange("p q r -> p (q r)"),
+                in_=a_grouped[:].rearrange("p q r v -> p (q r v)"),
+            )
+
+            acc = sums.tile([P, FEATURES], F32)
+            for q in range(PASSES):
+                nc.tensor.matmul_mx(
+                    out=acc[:],
+                    lhsT=a_codes[:, q, :].bitcast(FP8X4),
+                    lhsT_scale=a_scales[:, q, :],
+                    rhs=x_codes[:, q, :].bitcast(FP8X4),
+                    rhs_scale=x_scales[:, q, :],
+                    start=(q == 0),
+                    stop=(q == PASSES - 1),
+                )
+            y = work.tile([P, FEATURES], F32)
+            nc.vector.tensor_tensor(out=y[:], in0=acc[:], in1=bias[:, j, :], op=ADD)
+            nc.vector.tensor_scalar_max(out=y[:], in0=y[:], scalar1=0.0)
+            nc.sync.dma_start(out=out_blocks[j], in_=y[:])

@@ -21,6 +21,9 @@ ROWS = NODES * STEPS
 BLOCKS = ROWS // P
 PASSES = 2
 PLANES = 2
+RUN = 2
+ROUNDS = BLOCKS // RUN
+BEHIND = 2 // RUN
 
 FLOPS = 2 * ROWS * K * FEATURES
 
@@ -33,23 +36,27 @@ def tile_gcnfast_s_kernel(tc, h, e, AA_mask, GCW, GCB, out):
     out_blocks = out[0].rearrange("(pl j) t d -> j t pl d", j=BLOCKS)
 
     with ExitStack() as ctx:
+        ctx.enter_context(tc.manual_schedule())
         keep = ctx.enter_context(tc.tile_pool(name="keep", bufs=1))
         loads = ctx.enter_context(tc.tile_pool(name="loads", bufs=BLOCKS))
-        work = ctx.enter_context(tc.tile_pool(name="work", bufs=3))
+        work = ctx.enter_context(tc.tile_pool(name="work", bufs=8))
         flipped = ctx.enter_context(tc.psum_pool(name="flipped", bufs=6))
         sums = ctx.enter_context(tc.psum_pool(name="sums", bufs=2))
 
         x_raw = keep.tile([P, 2, 4 * FEATURES], BF16)
-        for tx in range(4):
-            nc.scalar.dma_start(
-                out=x_raw[32 * tx : 32 * tx + 32, :, :],
-                in_=h[0, :, 4 * tx : 4 * tx + 4, :].rearrange("(cp ce) tl d -> cp ce (tl d)", ce=2),
-            )
+        x_grouped = keep.tile([P, PASSES, FEATURES, 4], BF16, align_bytes=64)
+        x_codes = keep.tile([P, PASSES, FEATURES], U32, align_bytes=64)
+        x_scales = keep.tile([P, PASSES, FEATURES], U8, align_bytes=64)
         bias = keep.tile([P, BLOCKS, FEATURES], BF16)
-        nc.scalar.dma_start(out=bias[:], in_=bias_rows)
+        identity = keep.tile([P, P], F32)
         weight_tiles = []
         mask_tiles = []
-        for j in range(BLOCKS):
+        products = {}
+        grouped_tiles = {}
+        accumulators = {}
+        results = {}
+
+        def load_block(j):
             weight = loads.tile([P, K], BF16)
             nc.sync.dma_start(out=weight[:], in_=weight_rows[:, j, :])
             mask = loads.tile([P, K], BF16)
@@ -57,25 +64,29 @@ def tile_gcnfast_s_kernel(tc, h, e, AA_mask, GCW, GCB, out):
             weight_tiles.append(weight)
             mask_tiles.append(mask)
 
-        identity = keep.tile([P, P], F32)
-        make_identity(nc, identity[:])
+        def load_x():
+            for tx in range(4):
+                nc.sync.dma_start(
+                    out=x_raw[32 * tx : 32 * tx + 32, :, :],
+                    in_=h[0, :, 4 * tx : 4 * tx + 4, :].rearrange(
+                        "(cp ce) tl d -> cp ce (tl d)", ce=2
+                    ),
+                )
 
-        x_grouped = keep.tile([P, PASSES, FEATURES, 4], BF16, align_bytes=64)
-        x_steps = x_raw[:].rearrange("p ce (u q d) -> p q d u ce", u=PLANES, q=PASSES)
-        for q in range(PASSES):
-            nc.vector.tensor_copy(
-                out=x_grouped[:, q, :, :].rearrange("p d (u ce) -> p d u ce", ce=2),
-                in_=x_steps[:, q, :, :, :],
+        def prepare_x():
+            x_steps = x_raw[:].rearrange("p ce (u q d) -> p q d u ce", u=PLANES, q=PASSES)
+            for q in range(PASSES):
+                nc.vector.tensor_copy(
+                    out=x_grouped[:, q, :, :].rearrange("p d (u ce) -> p d u ce", ce=2),
+                    in_=x_steps[:, q, :, :, :],
+                )
+            nc.vector.quantize_mx(
+                out=x_codes[:].rearrange("p q d -> p (q d)").bitcast(FP8X4),
+                scales=x_scales[:].rearrange("p q d -> p (q d)"),
+                in_=x_grouped[:].rearrange("p q d v -> p (q d v)"),
             )
-        x_codes = keep.tile([P, PASSES, FEATURES], U32, align_bytes=64)
-        x_scales = keep.tile([P, PASSES, FEATURES], U8, align_bytes=64)
-        nc.vector.quantize_mx(
-            out=x_codes[:].rearrange("p q d -> p (q d)").bitcast(FP8X4),
-            scales=x_scales[:].rearrange("p q d -> p (q d)"),
-            in_=x_grouped[:].rearrange("p q d v -> p (q d v)"),
-        )
 
-        for j in range(BLOCKS):
+        def multiply_by_mask(j):
             product = work.tile([P, K], BF16)
             nc.vector.tensor_tensor(
                 out=product[:].rearrange("p (tl tx c) -> p tx tl c", tl=4, tx=4),
@@ -83,41 +94,78 @@ def tile_gcnfast_s_kernel(tc, h, e, AA_mask, GCW, GCB, out):
                 in1=mask_tiles[j][:].rearrange("p (tx tl c) -> p tx tl c", tx=4, tl=4),
                 op=MULT,
             )
-            product_words = product[:].bitcast(F32)
+            products[j] = product
 
-            a_grouped = work.tile([P, PASSES, P, 4], BF16, align_bytes=64)
-            for q in range(PASSES):
-                turned = flipped.tile([P, PLANES, P], F32)
-                for u in range(PLANES):
-                    tl = PASSES * u + q
-                    nc.tensor.transpose(
-                        turned[:, u, :], product_words[:, P * tl : P * tl + P], identity[:]
-                    )
-                nc.scalar.activation(
-                    out=a_grouped[:, q, :, :].rearrange("p r (u ce) -> p r u ce", ce=2),
-                    in_=turned[:].bitcast(BF16).rearrange("p u (r ce) -> p r u ce", ce=2),
-                    func=RELU,
+        def turn(j, q):
+            product_words = products[j][:].bitcast(F32)
+            turned = flipped.tile([P, PLANES, P], F32)
+            for u in range(PLANES):
+                tl = PASSES * u + q
+                nc.tensor.transpose(
+                    turned[:, u, :], product_words[:, P * tl : P * tl + P], identity[:]
                 )
-            a_codes = work.tile([P, PASSES, P], U32, align_bytes=64)
-            a_scales = work.tile([P, PASSES, P], U8, align_bytes=64)
+            a_grouped = work.tile([P, P, 4], BF16, align_bytes=64)
+            nc.scalar.activation(
+                out=a_grouped[:].rearrange("p r (u ce) -> p r u ce", ce=2),
+                in_=turned[:].bitcast(BF16).rearrange("p u (r ce) -> p r u ce", ce=2),
+                func=RELU,
+            )
+            grouped_tiles[(j, q)] = a_grouped
+
+        def quantise_and_multiply(j, q):
+            a_codes = work.tile([P, P], U32, align_bytes=64)
+            a_scales = work.tile([P, P], U8, align_bytes=64)
             nc.vector.quantize_mx(
-                out=a_codes[:].rearrange("p q r -> p (q r)").bitcast(FP8X4),
-                scales=a_scales[:].rearrange("p q r -> p (q r)"),
-                in_=a_grouped[:].rearrange("p q r v -> p (q r v)"),
+                out=a_codes[:].bitcast(FP8X4),
+                scales=a_scales[:],
+                in_=grouped_tiles[(j, q)][:].rearrange("p r v -> p (r v)"),
+            )
+            if q == 0:
+                acc = sums.tile([P, FEATURES], F32)
+                accumulators[j] = acc
+            nc.tensor.matmul_mx(
+                out=accumulators[j][:],
+                lhsT=a_codes[:].bitcast(FP8X4),
+                lhsT_scale=a_scales[:],
+                rhs=x_codes[:, q, :].bitcast(FP8X4),
+                rhs_scale=x_scales[:, q, :],
+                start=(q == 0),
+                stop=(q == PASSES - 1),
             )
 
-            acc = sums.tile([P, FEATURES], F32)
-            for q in range(PASSES):
-                nc.tensor.matmul_mx(
-                    out=acc[:],
-                    lhsT=a_codes[:, q, :].bitcast(FP8X4),
-                    lhsT_scale=a_scales[:, q, :],
-                    rhs=x_codes[:, q, :].bitcast(FP8X4),
-                    rhs_scale=x_scales[:, q, :],
-                    start=(q == 0),
-                    stop=(q == PASSES - 1),
-                )
+        def add_bias(j):
             y = work.tile([P, FEATURES], F32)
-            nc.vector.tensor_tensor(out=y[:], in0=acc[:], in1=bias[:, j, :], op=ADD)
-            nc.vector.tensor_scalar_max(out=y[:], in0=y[:], scalar1=0.0)
-            nc.sync.dma_start(out=out_blocks[j], in_=y[:])
+            nc.vector.tensor_tensor(out=y[:], in0=accumulators[j][:], in1=bias[:, j, :], op=ADD)
+            results[j] = y
+
+        def relu_and_store(j):
+            nc.vector.tensor_scalar_max(out=results[j][:], in0=results[j][:], scalar1=0.0)
+            nc.sync.dma_start(out=out_blocks[j], in_=results[j][:])
+
+        def blocks_of(r):
+            if 0 <= r < ROUNDS:
+                return range(RUN * r, RUN * r + RUN)
+            return range(0)
+
+        load_block(0)
+        load_x()
+        load_block(1)
+        nc.sync.dma_start(out=bias[:], in_=bias_rows)
+        for j in range(2, BLOCKS):
+            load_block(j)
+        make_identity(nc, identity[:])
+
+        for r in range(ROUNDS + BEHIND + 1):
+            for j in blocks_of(r):
+                multiply_by_mask(j)
+                if j == 0:
+                    prepare_x()
+                for q in range(PASSES):
+                    turn(j, q)
+            for j in blocks_of(r - BEHIND - 1):
+                add_bias(j)
+            for j in blocks_of(r - BEHIND - 1):
+                relu_and_store(j)
+            for j in blocks_of(r - BEHIND):
+                for q in range(PASSES):
+                    quantise_and_multiply(j, q)

@@ -24,6 +24,7 @@ PLANES = 2
 RUN = 2
 ROUNDS = BLOCKS // RUN
 BEHIND = 2 // RUN
+VECTOR_EVERY = 4
 
 FLOPS = 2 * ROWS * K * FEATURES
 
@@ -52,6 +53,7 @@ def tile_gcnfast_s_kernel(tc, h, e, AA_mask, GCW, GCB, out):
         weight_tiles = []
         mask_tiles = []
         products = {}
+        turned_tiles = {}
         grouped_tiles = {}
         accumulators = {}
         results = {}
@@ -104,12 +106,19 @@ def tile_gcnfast_s_kernel(tc, h, e, AA_mask, GCW, GCB, out):
                 nc.tensor.transpose(
                     turned[:, u, :], product_words[:, P * tl : P * tl + P], identity[:]
                 )
+            turned_tiles[(j, q)] = turned
+
+        def vector_empties(j, q):
+            return q == 0 and j % VECTOR_EVERY == VECTOR_EVERY - 1
+
+        def relu_out_of_psum(j, q):
             a_grouped = work.tile([P, P, 4], BF16, align_bytes=64)
-            nc.scalar.activation(
-                out=a_grouped[:].rearrange("p r (u ce) -> p r u ce", ce=2),
-                in_=turned[:].bitcast(BF16).rearrange("p u (r ce) -> p r u ce", ce=2),
-                func=RELU,
-            )
+            target = a_grouped[:].rearrange("p r (u ce) -> p r u ce", ce=2)
+            source = turned_tiles[(j, q)][:].bitcast(BF16).rearrange("p u (r ce) -> p r u ce", ce=2)
+            if vector_empties(j, q):
+                nc.vector.tensor_scalar_max(out=target, in0=source, scalar1=0.0)
+            else:
+                nc.scalar.activation(out=target, in_=source, func=RELU)
             grouped_tiles[(j, q)] = a_grouped
 
         def quantise_and_multiply(j, q):
@@ -162,10 +171,16 @@ def tile_gcnfast_s_kernel(tc, h, e, AA_mask, GCW, GCB, out):
                     prepare_x()
                 for q in range(PASSES):
                     turn(j, q)
+                    if not vector_empties(j, q):
+                        relu_out_of_psum(j, q)
             for j in blocks_of(r - BEHIND - 1):
                 add_bias(j)
             for j in blocks_of(r - BEHIND - 1):
                 relu_and_store(j)
+            for j in blocks_of(r):
+                for q in range(PASSES):
+                    if vector_empties(j, q):
+                        relu_out_of_psum(j, q)
             for j in blocks_of(r - BEHIND):
                 for q in range(PASSES):
                     quantise_and_multiply(j, q)

@@ -24,7 +24,6 @@ PLANES = 2
 RUN = 2
 ROUNDS = BLOCKS // RUN
 BEHIND = 2 // RUN
-VECTOR_EVERY = 4
 
 FLOPS = 2 * ROWS * K * FEATURES
 
@@ -53,7 +52,6 @@ def tile_gcnfast_s_kernel(tc, h, e, AA_mask, GCW, GCB, out):
         weight_tiles = []
         mask_tiles = []
         products = {}
-        turned_tiles = {}
         grouped_tiles = {}
         accumulators = {}
         results = {}
@@ -106,19 +104,12 @@ def tile_gcnfast_s_kernel(tc, h, e, AA_mask, GCW, GCB, out):
                 nc.tensor.transpose(
                     turned[:, u, :], product_words[:, P * tl : P * tl + P], identity[:]
                 )
-            turned_tiles[(j, q)] = turned
-
-        def vector_empties(j, q):
-            return q == 0 and j % VECTOR_EVERY == VECTOR_EVERY - 1
-
-        def relu_out_of_psum(j, q):
             a_grouped = work.tile([P, P, 4], BF16, align_bytes=64)
-            target = a_grouped[:].rearrange("p r (u ce) -> p r u ce", ce=2)
-            source = turned_tiles[(j, q)][:].bitcast(BF16).rearrange("p u (r ce) -> p r u ce", ce=2)
-            if vector_empties(j, q):
-                nc.vector.tensor_scalar_max(out=target, in0=source, scalar1=0.0)
-            else:
-                nc.scalar.activation(out=target, in_=source, func=RELU)
+            nc.scalar.activation(
+                out=a_grouped[:].rearrange("p r (u ce) -> p r u ce", ce=2),
+                in_=turned[:].bitcast(BF16).rearrange("p u (r ce) -> p r u ce", ce=2),
+                func=RELU,
+            )
             grouped_tiles[(j, q)] = a_grouped
 
         def quantise_and_multiply(j, q):
@@ -148,7 +139,7 @@ def tile_gcnfast_s_kernel(tc, h, e, AA_mask, GCW, GCB, out):
             results[j] = y
 
         def relu_and_store(j):
-            nc.vector.tensor_scalar_max(out=results[j][:], in0=results[j][:], scalar1=0.0)
+            nc.scalar.activation(out=results[j][:], in_=results[j][:], func=RELU)
             nc.sync.dma_start(out=out_blocks[j], in_=results[j][:])
 
         def blocks_of(r):
@@ -171,16 +162,10 @@ def tile_gcnfast_s_kernel(tc, h, e, AA_mask, GCW, GCB, out):
                     prepare_x()
                 for q in range(PASSES):
                     turn(j, q)
-                    if not vector_empties(j, q):
-                        relu_out_of_psum(j, q)
             for j in blocks_of(r - BEHIND - 1):
                 add_bias(j)
             for j in blocks_of(r - BEHIND - 1):
                 relu_and_store(j)
-            for j in blocks_of(r):
-                for q in range(PASSES):
-                    if vector_empties(j, q):
-                        relu_out_of_psum(j, q)
             for j in blocks_of(r - BEHIND):
                 for q in range(PASSES):
                     quantise_and_multiply(j, q)

@@ -21,9 +21,9 @@ ROWS = NODES * STEPS
 BLOCKS = ROWS // P
 PASSES = 2
 PLANES = 2
-RUN = 2
-ROUNDS = BLOCKS // RUN
-BEHIND = 2 // RUN
+QUANTISE_BEHIND = 2
+ADD_BEHIND = 4
+STORE_BEHIND = 5
 
 FLOPS = 2 * ROWS * K * FEATURES
 
@@ -40,8 +40,8 @@ def tile_gcnfast_s_kernel(tc, h, e, AA_mask, GCW, GCB, out):
         keep = ctx.enter_context(tc.tile_pool(name="keep", bufs=1))
         loads = ctx.enter_context(tc.tile_pool(name="loads", bufs=BLOCKS))
         work = ctx.enter_context(tc.tile_pool(name="work", bufs=8))
-        flipped = ctx.enter_context(tc.psum_pool(name="flipped", bufs=6))
-        sums = ctx.enter_context(tc.psum_pool(name="sums", bufs=2))
+        flipped = ctx.enter_context(tc.psum_pool(name="flipped", bufs=5))
+        sums = ctx.enter_context(tc.psum_pool(name="sums", bufs=3))
 
         x_raw = keep.tile([P, 2, 4 * FEATURES], BF16)
         x_grouped = keep.tile([P, PASSES, FEATURES, 4], BF16, align_bytes=64)
@@ -52,6 +52,7 @@ def tile_gcnfast_s_kernel(tc, h, e, AA_mask, GCW, GCB, out):
         weight_tiles = []
         mask_tiles = []
         products = {}
+        turned_tiles = {}
         grouped_tiles = {}
         accumulators = {}
         results = {}
@@ -99,18 +100,25 @@ def tile_gcnfast_s_kernel(tc, h, e, AA_mask, GCW, GCB, out):
         def turn(j, q):
             product_words = products[j][:].bitcast(F32)
             turned = flipped.tile([P, PLANES, P], F32)
+            turned_tiles[(j, q)] = turned
             for u in range(PLANES):
                 tl = PASSES * u + q
                 nc.tensor.transpose(
                     turned[:, u, :], product_words[:, P * tl : P * tl + P], identity[:]
                 )
+
+        def empty(j, q):
             a_grouped = work.tile([P, P, 4], BF16, align_bytes=64)
-            nc.scalar.activation(
-                out=a_grouped[:].rearrange("p r (u ce) -> p r u ce", ce=2),
-                in_=turned[:].bitcast(BF16).rearrange("p u (r ce) -> p r u ce", ce=2),
-                func=RELU,
-            )
+            out = a_grouped[:].rearrange("p r (u ce) -> p r u ce", ce=2)
+            in_ = turned_tiles[(j, q)][:].bitcast(BF16).rearrange("p u (r ce) -> p r u ce", ce=2)
+            if on_vector(j, q):
+                nc.vector.tensor_scalar_max(out, in_, 0.0)
+            else:
+                nc.scalar.activation(out=out, in_=in_, func=RELU)
             grouped_tiles[(j, q)] = a_grouped
+
+        def on_vector(j, q):
+            return j == BLOCKS - 1 and q == PASSES - 1
 
         def quantise_and_multiply(j, q):
             a_codes = work.tile([P, P], U32, align_bytes=64)
@@ -142,30 +150,34 @@ def tile_gcnfast_s_kernel(tc, h, e, AA_mask, GCW, GCB, out):
             nc.scalar.activation(out=results[j][:], in_=results[j][:], func=RELU)
             nc.sync.dma_start(out=out_blocks[j], in_=results[j][:])
 
-        def blocks_of(r):
-            if 0 <= r < ROUNDS:
-                return range(RUN * r, RUN * r + RUN)
-            return range(0)
-
         load_block(0)
         load_x()
-        load_block(1)
-        nc.sync.dma_start(out=bias[:], in_=bias_rows)
-        for j in range(2, BLOCKS):
+        for j in range(1, BLOCKS):
+            if j == ADD_BEHIND - 1:
+                nc.sync.dma_start(out=bias[:], in_=bias_rows)
             load_block(j)
         make_identity(nc, identity[:])
 
-        for r in range(ROUNDS + BEHIND + 1):
-            for j in blocks_of(r):
-                multiply_by_mask(j)
-                if j == 0:
+        for step in range(BLOCKS + STORE_BEHIND):
+            if step < BLOCKS:
+                multiply_by_mask(step)
+                if step == 0:
                     prepare_x()
                 for q in range(PASSES):
-                    turn(j, q)
-            for j in blocks_of(r - BEHIND - 1):
-                add_bias(j)
-            for j in blocks_of(r - BEHIND - 1):
-                relu_and_store(j)
-            for j in blocks_of(r - BEHIND):
+                    turn(step, q)
+                    if not on_vector(step, q):
+                        empty(step, q)
+            j = step - QUANTISE_BEHIND
+            if 0 <= j < BLOCKS:
                 for q in range(PASSES):
                     quantise_and_multiply(j, q)
+            j = step - ADD_BEHIND
+            if 0 <= j < BLOCKS:
+                add_bias(j)
+            if step < BLOCKS:
+                for q in range(PASSES):
+                    if on_vector(step, q):
+                        empty(step, q)
+            j = step - STORE_BEHIND
+            if 0 <= j < BLOCKS:
+                relu_and_store(j)

@@ -21,9 +21,11 @@ ROWS = NODES * STEPS
 BLOCKS = ROWS // P
 PASSES = 2
 PLANES = 2
+LAST = BLOCKS - 1
 QUANTISE_BEHIND = 2
-ADD_BEHIND = 4
-STORE_BEHIND = 5
+ON_VECTOR = ((5, 1),)
+GROUPS = ((0, 1, 2, 3), (4, 5), (6,), (7,))
+FIRSTS = {group[0]: len(group) for group in GROUPS}
 
 FLOPS = 2 * ROWS * K * FEATURES
 
@@ -54,8 +56,10 @@ def tile_gcnfast_s_kernel(tc, h, e, AA_mask, GCW, GCB, out):
         products = {}
         turned_tiles = {}
         grouped_tiles = {}
+        code_tiles = {}
+        scale_tiles = {}
         accumulators = {}
-        results = {}
+        outputs = {}
 
         def load_block(j):
             weight = loads.tile([P, K], BF16)
@@ -74,18 +78,28 @@ def tile_gcnfast_s_kernel(tc, h, e, AA_mask, GCW, GCB, out):
                     ),
                 )
 
-        def prepare_x():
+        def group_x():
             x_steps = x_raw[:].rearrange("p ce (u q d) -> p q d u ce", u=PLANES, q=PASSES)
             for q in range(PASSES):
                 nc.vector.tensor_copy(
                     out=x_grouped[:, q, :, :].rearrange("p d (u ce) -> p d u ce", ce=2),
                     in_=x_steps[:, q, :, :, :],
                 )
+
+        def quantise_x():
             nc.vector.quantize_mx(
                 out=x_codes[:].rearrange("p q d -> p (q d)").bitcast(FP8X4),
                 scales=x_scales[:].rearrange("p q d -> p (q d)"),
                 in_=x_grouped[:].rearrange("p q d v -> p (q d v)"),
             )
+
+        def start_block(j):
+            grouped = work.tile([P, PASSES, P, 4], BF16, align_bytes=64)
+            grouped_tiles[j] = grouped
+            codes = work.tile([P, PASSES, P], U32, align_bytes=64)
+            code_tiles[j] = codes
+            scales = work.tile([P, PASSES, P], U8, align_bytes=64)
+            scale_tiles[j] = scales
 
         def multiply_by_mask(j):
             product = work.tile([P, K], BF16)
@@ -95,89 +109,120 @@ def tile_gcnfast_s_kernel(tc, h, e, AA_mask, GCW, GCB, out):
                 in1=mask_tiles[j][:].rearrange("p (tx tl c) -> p tx tl c", tx=4, tl=4),
                 op=MULT,
             )
-            products[j] = product
+            for q in range(PASSES):
+                for u in range(PLANES):
+                    tl = PASSES * u + q
+                    products[(j, q, u)] = product[:, 2 * P * tl : 2 * P * tl + 2 * P]
+
+        def multiply_half_by_mask(j, q):
+            product = work.tile([P, PLANES, 2 * P], BF16)
+            nc.vector.tensor_tensor(
+                out=product[:].rearrange("p u (tx c) -> p tx u c", tx=4),
+                in0=weight_tiles[j][:].rearrange("p (tx u q c) -> p q tx u c", tx=4, u=PLANES, q=PASSES)[:, q],
+                in1=mask_tiles[j][:].rearrange("p (tx u q c) -> p q tx u c", tx=4, u=PLANES, q=PASSES)[:, q],
+                op=MULT,
+            )
+            for u in range(PLANES):
+                products[(j, q, u)] = product[:, u, :]
 
         def turn(j, q):
-            product_words = products[j][:].bitcast(F32)
             turned = flipped.tile([P, PLANES, P], F32)
             turned_tiles[(j, q)] = turned
             for u in range(PLANES):
-                tl = PASSES * u + q
                 nc.tensor.transpose(
-                    turned[:, u, :], product_words[:, P * tl : P * tl + P], identity[:]
+                    turned[:, u, :], products[(j, q, u)].bitcast(F32), identity[:]
                 )
 
         def empty(j, q):
-            a_grouped = work.tile([P, P, 4], BF16, align_bytes=64)
-            out = a_grouped[:].rearrange("p r (u ce) -> p r u ce", ce=2)
+            out = grouped_tiles[j][:, q, :, :].rearrange("p r (u ce) -> p r u ce", ce=2)
             in_ = turned_tiles[(j, q)][:].bitcast(BF16).rearrange("p u (r ce) -> p r u ce", ce=2)
-            if on_vector(j, q):
+            if (j, q) in ON_VECTOR:
                 nc.vector.tensor_scalar_max(out, in_, 0.0)
             else:
                 nc.scalar.activation(out=out, in_=in_, func=RELU)
-            grouped_tiles[(j, q)] = a_grouped
 
-        def on_vector(j, q):
-            return j == BLOCKS - 1 and q == PASSES - 1
-
-        def quantise_and_multiply(j, q):
-            a_codes = work.tile([P, P], U32, align_bytes=64)
-            a_scales = work.tile([P, P], U8, align_bytes=64)
+        def quantise(j, passes):
             nc.vector.quantize_mx(
-                out=a_codes[:].bitcast(FP8X4),
-                scales=a_scales[:],
-                in_=grouped_tiles[(j, q)][:].rearrange("p r v -> p (r v)"),
+                out=code_tiles[j][:, passes, :].rearrange("p q r -> p (q r)").bitcast(FP8X4),
+                scales=scale_tiles[j][:, passes, :].rearrange("p q r -> p (q r)"),
+                in_=grouped_tiles[j][:, passes, :, :].rearrange("p q r v -> p (q r v)"),
             )
-            if q == 0:
-                acc = sums.tile([P, FEATURES], F32)
-                accumulators[j] = acc
+
+        def multiply(j, q):
+            if q == 0 and j in FIRSTS:
+                acc = sums.tile([P, FIRSTS[j], FEATURES], F32)
+                for i in range(FIRSTS[j]):
+                    accumulators[j + i] = acc[:, i, :]
+                accumulators[(j, "all")] = acc
             nc.tensor.matmul_mx(
-                out=accumulators[j][:],
-                lhsT=a_codes[:].bitcast(FP8X4),
-                lhsT_scale=a_scales[:],
+                out=accumulators[j],
+                lhsT=code_tiles[j][:, q, :].bitcast(FP8X4),
+                lhsT_scale=scale_tiles[j][:, q, :],
                 rhs=x_codes[:, q, :].bitcast(FP8X4),
                 rhs_scale=x_scales[:, q, :],
                 start=(q == 0),
                 stop=(q == PASSES - 1),
             )
 
-        def add_bias(j):
-            y = work.tile([P, FEATURES], F32)
-            nc.vector.tensor_tensor(out=y[:], in0=accumulators[j][:], in1=bias[:, j, :], op=ADD)
-            results[j] = y
+        def add_bias(group):
+            first = group[0]
+            y = work.tile([P, len(group), FEATURES], F32)
+            nc.vector.tensor_tensor(
+                out=y[:],
+                in0=accumulators[(first, "all")][:],
+                in1=bias[:, first : first + len(group), :],
+                op=ADD,
+            )
+            outputs[group] = y
 
-        def relu_and_store(j):
-            nc.scalar.activation(out=results[j][:], in_=results[j][:], func=RELU)
-            nc.sync.dma_start(out=out_blocks[j], in_=results[j][:])
+        def relu_and_store(group):
+            y = outputs[group]
+            nc.scalar.activation(out=y[:], in_=y[:], func=RELU)
+            for j in group:
+                nc.sync.dma_start(out=out_blocks[j], in_=y[:, j - group[0], :])
 
         load_block(0)
         load_x()
         for j in range(1, BLOCKS):
-            if j == ADD_BEHIND - 1:
-                nc.sync.dma_start(out=bias[:], in_=bias_rows)
             load_block(j)
+        nc.sync.dma_start(out=bias[:], in_=bias_rows)
         make_identity(nc, identity[:])
 
-        for step in range(BLOCKS + STORE_BEHIND):
+        for step in range(BLOCKS + 2):
             if step < BLOCKS:
-                multiply_by_mask(step)
-                if step == 0:
-                    prepare_x()
+                start_block(step)
+                if step < LAST:
+                    multiply_by_mask(step)
                 for q in range(PASSES):
+                    if step == LAST:
+                        multiply_half_by_mask(step, q)
                     turn(step, q)
-                    if not on_vector(step, q):
+                    if (step, q) not in ON_VECTOR:
                         empty(step, q)
+                if step == 0:
+                    group_x()
+                if step == 1:
+                    quantise_x()
+                for q in range(PASSES):
+                    if (step - 1, q) in ON_VECTOR:
+                        empty(step - 1, q)
             j = step - QUANTISE_BEHIND
-            if 0 <= j < BLOCKS:
+            if 0 <= j < LAST:
+                quantise(j, slice(0, PASSES))
                 for q in range(PASSES):
-                    quantise_and_multiply(j, q)
-            j = step - ADD_BEHIND
-            if 0 <= j < BLOCKS:
-                add_bias(j)
-            if step < BLOCKS:
-                for q in range(PASSES):
-                    if on_vector(step, q):
-                        empty(step, q)
-            j = step - STORE_BEHIND
-            if 0 <= j < BLOCKS:
-                relu_and_store(j)
+                    multiply(j, q)
+            if step == LAST:
+                add_bias(GROUPS[0])
+                relu_and_store(GROUPS[0])
+            if step == LAST + 1:
+                quantise(LAST, slice(0, 1))
+                multiply(LAST, 0)
+                add_bias(GROUPS[1])
+                relu_and_store(GROUPS[1])
+            if step == LAST + 2:
+                quantise(LAST, slice(1, 2))
+                multiply(LAST, 1)
+                add_bias(GROUPS[2])
+                relu_and_store(GROUPS[2])
+                add_bias(GROUPS[3])
+                relu_and_store(GROUPS[3])

@@ -22,8 +22,10 @@ BLOCKS = ROWS // P
 PASSES = 2
 PLANES = 2
 LAST = BLOCKS - 1
+X_BEFORE = 2
 QUANTISE_BEHIND = 2
-ON_VECTOR = ((5, 1),)
+ON_VECTOR = ((4, 1), (7, 1))
+HALVED = (6, 7)
 GROUPS = ((0, 1, 2, 3), (4, 5), (6,), (7,))
 FIRSTS = {group[0]: len(group) for group in GROUPS}
 
@@ -177,13 +179,16 @@ def tile_gcnfast_s_kernel(tc, h, e, AA_mask, GCW, GCB, out):
 
         def relu_and_store(group):
             y = outputs[group]
-            nc.scalar.activation(out=y[:], in_=y[:], func=RELU)
+            if group == GROUPS[-1]:
+                nc.vector.tensor_scalar_max(y[:], y[:], 0.0)
+            else:
+                nc.scalar.activation(out=y[:], in_=y[:], func=RELU)
             for j in group:
                 nc.sync.dma_start(out=out_blocks[j], in_=y[:, j - group[0], :])
 
-        load_block(0)
-        load_x()
-        for j in range(1, BLOCKS):
+        for j in range(BLOCKS):
+            if j == X_BEFORE:
+                load_x()
             load_block(j)
         nc.sync.dma_start(out=bias[:], in_=bias_rows)
         make_identity(nc, identity[:])
@@ -191,37 +196,35 @@ def tile_gcnfast_s_kernel(tc, h, e, AA_mask, GCW, GCB, out):
         for step in range(BLOCKS + 2):
             if step < BLOCKS:
                 start_block(step)
-                if step < LAST:
+                if step not in HALVED:
                     multiply_by_mask(step)
                 for q in range(PASSES):
-                    if step == LAST:
+                    if step in HALVED:
                         multiply_half_by_mask(step, q)
                     turn(step, q)
                     if (step, q) not in ON_VECTOR:
                         empty(step, q)
-                if step == 0:
+                if step == X_BEFORE - 1:
                     group_x()
-                if step == 1:
+                if step == X_BEFORE:
                     quantise_x()
                 for q in range(PASSES):
                     if (step - 1, q) in ON_VECTOR:
                         empty(step - 1, q)
             j = step - QUANTISE_BEHIND
-            if 0 <= j < LAST:
-                quantise(j, slice(0, PASSES))
-                for q in range(PASSES):
-                    multiply(j, q)
+            if j < 0:
+                continue
+            for q in range(PASSES):
+                quantise(j, slice(q, q + 1))
+                multiply(j, q)
             if step == LAST:
                 add_bias(GROUPS[0])
                 relu_and_store(GROUPS[0])
+                empty(LAST, 1)
             if step == LAST + 1:
-                quantise(LAST, slice(0, 1))
-                multiply(LAST, 0)
                 add_bias(GROUPS[1])
                 relu_and_store(GROUPS[1])
             if step == LAST + 2:
-                quantise(LAST, slice(1, 2))
-                multiply(LAST, 1)
                 add_bias(GROUPS[2])
                 relu_and_store(GROUPS[2])
                 add_bias(GROUPS[3])

@@ -24,7 +24,7 @@ PLANES = 2
 LAST = BLOCKS - 1
 X_BEFORE = 2
 QUANTISE_BEHIND = 2
-ON_VECTOR = ((4, 1), (7, 1))
+RECTIFIED = (5, 7)
 HALVED = (6, 7)
 GROUPS = ((0, 1, 2, 3), (4, 5), (6,), (7,))
 FIRSTS = {group[0]: len(group) for group in GROUPS}
@@ -44,8 +44,8 @@ def tile_gcnfast_s_kernel(tc, h, e, AA_mask, GCW, GCB, out):
         keep = ctx.enter_context(tc.tile_pool(name="keep", bufs=1))
         loads = ctx.enter_context(tc.tile_pool(name="loads", bufs=BLOCKS))
         work = ctx.enter_context(tc.tile_pool(name="work", bufs=8))
-        flipped = ctx.enter_context(tc.psum_pool(name="flipped", bufs=5))
-        sums = ctx.enter_context(tc.psum_pool(name="sums", bufs=3))
+        flipped = ctx.enter_context(tc.psum_pool(name="flipped", bufs=6))
+        sums = ctx.enter_context(tc.psum_pool(name="sums", bufs=2))
 
         x_raw = keep.tile([P, 2, 4 * FEATURES], BF16)
         x_grouped = keep.tile([P, PASSES, FEATURES, 4], BF16, align_bytes=64)
@@ -103,6 +103,11 @@ def tile_gcnfast_s_kernel(tc, h, e, AA_mask, GCW, GCB, out):
             scales = work.tile([P, PASSES, P], U8, align_bytes=64)
             scale_tiles[j] = scales
 
+        def rectify(j):
+            rectified = work.tile([P, K], BF16)
+            nc.vector.tensor_scalar_max(rectified[:], weight_tiles[j][:], 0.0)
+            weight_tiles[j] = rectified
+
         def multiply_by_mask(j):
             product = work.tile([P, K], BF16)
             nc.vector.tensor_tensor(
@@ -136,12 +141,21 @@ def tile_gcnfast_s_kernel(tc, h, e, AA_mask, GCW, GCB, out):
                 )
 
         def empty(j, q):
-            out = grouped_tiles[j][:, q, :, :].rearrange("p r (u ce) -> p r u ce", ce=2)
-            in_ = turned_tiles[(j, q)][:].bitcast(BF16).rearrange("p u (r ce) -> p r u ce", ce=2)
-            if (j, q) in ON_VECTOR:
-                nc.vector.tensor_scalar_max(out, in_, 0.0)
+            grouped = grouped_tiles[j][:, q, :, :]
+            turned = turned_tiles[(j, q)][:]
+            if j in RECTIFIED:
+                nc.scalar.copy(
+                    out=grouped.rearrange("p r v -> p (r v)").bitcast(F32).rearrange(
+                        "p (r u) -> p r u", u=PLANES
+                    ),
+                    in_=turned.rearrange("p u r -> p r u"),
+                )
             else:
-                nc.scalar.activation(out=out, in_=in_, func=RELU)
+                nc.scalar.activation(
+                    out=grouped.rearrange("p r (u ce) -> p r u ce", ce=2),
+                    in_=turned.bitcast(BF16).rearrange("p u (r ce) -> p r u ce", ce=2),
+                    func=RELU,
+                )
 
         def quantise(j, passes):
             nc.vector.quantize_mx(
@@ -202,15 +216,13 @@ def tile_gcnfast_s_kernel(tc, h, e, AA_mask, GCW, GCB, out):
                     if step in HALVED:
                         multiply_half_by_mask(step, q)
                     turn(step, q)
-                    if (step, q) not in ON_VECTOR:
-                        empty(step, q)
+                    empty(step, q)
                 if step == X_BEFORE - 1:
                     group_x()
                 if step == X_BEFORE:
                     quantise_x()
-                for q in range(PASSES):
-                    if (step - 1, q) in ON_VECTOR:
-                        empty(step - 1, q)
+                if step + 1 in RECTIFIED:
+                    rectify(step + 1)
             j = step - QUANTISE_BEHIND
             if j < 0:
                 continue
@@ -220,7 +232,6 @@ def tile_gcnfast_s_kernel(tc, h, e, AA_mask, GCW, GCB, out):
             if step == LAST:
                 add_bias(GROUPS[0])
                 relu_and_store(GROUPS[0])
-                empty(LAST, 1)
             if step == LAST + 1:
                 add_bias(GROUPS[1])
                 relu_and_store(GROUPS[1])

@@ -26,7 +26,7 @@ X_BEFORE = 2
 QUANTISE_BEHIND = 2
 RECTIFIED = (5, 7)
 HALVED = (6, 7)
-GROUPS = ((0, 1, 2, 3), (4, 5), (6,), (7,))
+GROUPS = ((0, 1), (2, 3), (4,), (5,), (6,), (7,))
 FIRSTS = {group[0]: len(group) for group in GROUPS}
 
 FLOPS = 2 * ROWS * K * FEATURES
@@ -44,8 +44,8 @@ def tile_gcnfast_s_kernel(tc, h, e, AA_mask, GCW, GCB, out):
         keep = ctx.enter_context(tc.tile_pool(name="keep", bufs=1))
         loads = ctx.enter_context(tc.tile_pool(name="loads", bufs=BLOCKS))
         work = ctx.enter_context(tc.tile_pool(name="work", bufs=8))
-        flipped = ctx.enter_context(tc.psum_pool(name="flipped", bufs=6))
-        sums = ctx.enter_context(tc.psum_pool(name="sums", bufs=2))
+        flipped = ctx.enter_context(tc.psum_pool(name="flipped", bufs=5))
+        sums = ctx.enter_context(tc.psum_pool(name="sums", bufs=3))
 
         x_raw = keep.tile([P, 2, 4 * FEATURES], BF16)
         x_grouped = keep.tile([P, PASSES, FEATURES, 4], BF16, align_bytes=64)
@@ -230,13 +230,10 @@ def tile_gcnfast_s_kernel(tc, h, e, AA_mask, GCW, GCB, out):
                 quantise(j, slice(q, q + 1))
                 multiply(j, q)
             if step == LAST:
-                add_bias(GROUPS[0])
-                relu_and_store(GROUPS[0])
-            if step == LAST + 1:
-                add_bias(GROUPS[1])
-                relu_and_store(GROUPS[1])
+                for group in GROUPS[:3]:
+                    add_bias(group)
+                    relu_and_store(group)
             if step == LAST + 2:
-                add_bias(GROUPS[2])
-                relu_and_store(GROUPS[2])
-                add_bias(GROUPS[3])
-                relu_and_store(GROUPS[3])
+                for group in GROUPS[3:]:
+                    add_bias(group)
+                    relu_and_store(group)

@@ -226,9 +226,14 @@ def tile_gcnfast_s_kernel(tc, h, e, AA_mask, GCW, GCB, out):
             j = step - QUANTISE_BEHIND
             if j < 0:
                 continue
-            for q in range(PASSES):
-                quantise(j, slice(q, q + 1))
-                multiply(j, q)
+            if j < LAST:
+                quantise(j, slice(0, PASSES))
+                for q in range(PASSES):
+                    multiply(j, q)
+            else:
+                for q in range(PASSES):
+                    quantise(j, slice(q, q + 1))
+                    multiply(j, q)
             if step == LAST:
                 for group in GROUPS[:3]:
                     add_bias(group)

from contextlib import ExitStack

import concourse.mybir as mybir
from concourse.masks import make_identity

F32 = mybir.dt.float32
BF16 = mybir.dt.bfloat16
U32 = mybir.dt.uint32
U8 = mybir.dt.uint8
FP8X4 = mybir.dt.float8_e4m3fn_x4
RELU = mybir.ActivationFunctionType.Relu
MULT = mybir.AluOpType.mult
ADD = mybir.AluOpType.add

P = 128
NODES = 64
STEPS = 16
FEATURES = 128
K = NODES * STEPS
ROWS = NODES * STEPS
BLOCKS = ROWS // P
PASSES = 2
PLANES = 2
LAST = BLOCKS - 1
X_BEFORE = 2
QUANTISE_BEHIND = 2
RECTIFIED = (5, 7)
HALVED = (6, 7)
GROUPS = ((0, 1), (2, 3), (4,), (5,), (6,), (7,))
FIRSTS = {group[0]: len(group) for group in GROUPS}

FLOPS = 2 * ROWS * K * FEATURES


def tile_gcnfast_s_kernel(tc, h, e, AA_mask, GCW, GCB, out):
    nc = tc.nc
    weight_rows = GCW.rearrange("(p j) k -> p j k", j=BLOCKS)
    mask_rows = AA_mask.rearrange("(p j) k -> p j k", j=BLOCKS)
    bias_rows = GCB.rearrange("(p j) d -> p j d", j=BLOCKS)
    out_blocks = out[0].rearrange("(pl j) t d -> j t pl d", j=BLOCKS)

    with ExitStack() as ctx:
        ctx.enter_context(tc.manual_schedule())
        keep = ctx.enter_context(tc.tile_pool(name="keep", bufs=1))
        loads = ctx.enter_context(tc.tile_pool(name="loads", bufs=BLOCKS))
        work = ctx.enter_context(tc.tile_pool(name="work", bufs=8))
        flipped = ctx.enter_context(tc.psum_pool(name="flipped", bufs=5))
        sums = ctx.enter_context(tc.psum_pool(name="sums", bufs=3))

        x_raw = keep.tile([P, 2, 4 * FEATURES], BF16)
        x_grouped = keep.tile([P, PASSES, FEATURES, 4], BF16, align_bytes=64)
        x_codes = keep.tile([P, PASSES, FEATURES], U32, align_bytes=64)
        x_scales = keep.tile([P, PASSES, FEATURES], U8, align_bytes=64)
        bias = keep.tile([P, BLOCKS, FEATURES], BF16)
        identity = keep.tile([P, P], F32)
        weight_tiles = []
        mask_tiles = []
        products = {}
        turned_tiles = {}
        grouped_tiles = {}
        code_tiles = {}
        scale_tiles = {}
        accumulators = {}
        outputs = {}

        def load_block(j):
            weight = loads.tile([P, K], BF16)
            nc.sync.dma_start(out=weight[:], in_=weight_rows[:, j, :])
            mask = loads.tile([P, K], BF16)
            nc.sync.dma_start(out=mask[:], in_=mask_rows[:, j, :])
            weight_tiles.append(weight)
            mask_tiles.append(mask)

        def load_x():
            for tx in range(4):
                nc.sync.dma_start(
                    out=x_raw[32 * tx : 32 * tx + 32, :, :],
                    in_=h[0, :, 4 * tx : 4 * tx + 4, :].rearrange(
                        "(cp ce) tl d -> cp ce (tl d)", ce=2
                    ),
                )

        def group_x():
            x_steps = x_raw[:].rearrange("p ce (u q d) -> p q d u ce", u=PLANES, q=PASSES)
            for q in range(PASSES):
                nc.vector.tensor_copy(
                    out=x_grouped[:, q, :, :].rearrange("p d (u ce) -> p d u ce", ce=2),
                    in_=x_steps[:, q, :, :, :],
                )

        def quantise_x():
            nc.vector.quantize_mx(
                out=x_codes[:].rearrange("p q d -> p (q d)").bitcast(FP8X4),
                scales=x_scales[:].rearrange("p q d -> p (q d)"),
                in_=x_grouped[:].rearrange("p q d v -> p (q d v)"),
            )

        def start_block(j):
            grouped = work.tile([P, PASSES, P, 4], BF16, align_bytes=64)
            grouped_tiles[j] = grouped
            codes = work.tile([P, PASSES, P], U32, align_bytes=64)
            code_tiles[j] = codes
            scales = work.tile([P, PASSES, P], U8, align_bytes=64)
            scale_tiles[j] = scales

        def rectify(j):
            rectified = work.tile([P, K], BF16)
            nc.vector.tensor_scalar_max(rectified[:], weight_tiles[j][:], 0.0)
            weight_tiles[j] = rectified

        def multiply_by_mask(j):
            product = work.tile([P, K], BF16)
            nc.vector.tensor_tensor(
                out=product[:].rearrange("p (tl tx c) -> p tx tl c", tl=4, tx=4),
                in0=weight_tiles[j][:].rearrange("p (tx tl c) -> p tx tl c", tx=4, tl=4),
                in1=mask_tiles[j][:].rearrange("p (tx tl c) -> p tx tl c", tx=4, tl=4),
                op=MULT,
            )
            for q in range(PASSES):
                for u in range(PLANES):
                    tl = PASSES * u + q
                    products[(j, q, u)] = product[:, 2 * P * tl : 2 * P * tl + 2 * P]

        def multiply_half_by_mask(j, q):
            product = work.tile([P, PLANES, 2 * P], BF16)
            nc.vector.tensor_tensor(
                out=product[:].rearrange("p u (tx c) -> p tx u c", tx=4),
                in0=weight_tiles[j][:].rearrange("p (tx u q c) -> p q tx u c", tx=4, u=PLANES, q=PASSES)[:, q],
                in1=mask_tiles[j][:].rearrange("p (tx u q c) -> p q tx u c", tx=4, u=PLANES, q=PASSES)[:, q],
                op=MULT,
            )
            for u in range(PLANES):
                products[(j, q, u)] = product[:, u, :]

        def turn(j, q):
            turned = flipped.tile([P, PLANES, P], F32)
            turned_tiles[(j, q)] = turned
            for u in range(PLANES):
                nc.tensor.transpose(
                    turned[:, u, :], products[(j, q, u)].bitcast(F32), identity[:]
                )

        def empty(j, q):
            grouped = grouped_tiles[j][:, q, :, :]
            turned = turned_tiles[(j, q)][:]
            if j in RECTIFIED:
                nc.scalar.copy(
                    out=grouped.rearrange("p r v -> p (r v)").bitcast(F32).rearrange(
                        "p (r u) -> p r u", u=PLANES
                    ),
                    in_=turned.rearrange("p u r -> p r u"),
                )
            else:
                nc.scalar.activation(
                    out=grouped.rearrange("p r (u ce) -> p r u ce", ce=2),
                    in_=turned.bitcast(BF16).rearrange("p u (r ce) -> p r u ce", ce=2),
                    func=RELU,
                )

        def quantise(j, passes):
            nc.vector.quantize_mx(
                out=code_tiles[j][:, passes, :].rearrange("p q r -> p (q r)").bitcast(FP8X4),
                scales=scale_tiles[j][:, passes, :].rearrange("p q r -> p (q r)"),
                in_=grouped_tiles[j][:, passes, :, :].rearrange("p q r v -> p (q r v)"),
            )

        def multiply(j, q):
            if q == 0 and j in FIRSTS:
                acc = sums.tile([P, FIRSTS[j], FEATURES], F32)
                for i in range(FIRSTS[j]):
                    accumulators[j + i] = acc[:, i, :]
                accumulators[(j, "all")] = acc
            nc.tensor.matmul_mx(
                out=accumulators[j],
                lhsT=code_tiles[j][:, q, :].bitcast(FP8X4),
                lhsT_scale=scale_tiles[j][:, q, :],
                rhs=x_codes[:, q, :].bitcast(FP8X4),
                rhs_scale=x_scales[:, q, :],
                start=(q == 0),
                stop=(q == PASSES - 1),
            )

        def add_bias(group):
            first = group[0]
            y = work.tile([P, len(group), FEATURES], F32)
            nc.vector.tensor_tensor(
                out=y[:],
                in0=accumulators[(first, "all")][:],
                in1=bias[:, first : first + len(group), :],
                op=ADD,
            )
            outputs[group] = y

        def relu_and_store(group):
            y = outputs[group]
            if group == GROUPS[-1]:
                nc.vector.tensor_scalar_max(y[:], y[:], 0.0)
            else:
                nc.scalar.activation(out=y[:], in_=y[:], func=RELU)
            for j in group:
                nc.sync.dma_start(out=out_blocks[j], in_=y[:, j - group[0], :])

        for j in range(BLOCKS):
            if j == X_BEFORE:
                load_x()
            load_block(j)
        nc.sync.dma_start(out=bias[:], in_=bias_rows)
        make_identity(nc, identity[:])

        for step in range(BLOCKS + 2):
            if step < BLOCKS:
                start_block(step)
                if step not in HALVED:
                    multiply_by_mask(step)
                for q in range(PASSES):
                    if step in HALVED:
                        multiply_half_by_mask(step, q)
                    turn(step, q)
                    empty(step, q)
                if step == X_BEFORE - 1:
                    group_x()
                if step == X_BEFORE:
                    quantise_x()
                if step + 1 in RECTIFIED:
                    rectify(step + 1)
            j = step - QUANTISE_BEHIND
            if j < 0:
                continue
            if j < LAST:
                quantise(j, slice(0, PASSES))
                for q in range(PASSES):
                    multiply(j, q)
            else:
                for q in range(PASSES):
                    quantise(j, slice(q, q + 1))
                    multiply(j, q)
            if step == LAST:
                for group in GROUPS[:3]:
                    add_bias(group)
                    relu_and_store(group)
            if step == LAST + 2:
                for group in GROUPS[3:]:
                    add_bias(group)
                    relu_and_store(group)
